import numpy as np
import ml_dtypes


def mxq(x, axis, fmt="e4m3"):
    dtype, down = {"e4m3": (ml_dtypes.float8_e4m3fn, 7), "e5m2": (ml_dtypes.float8_e5m2, 14)}[fmt]
    v = np.moveaxis(np.asarray(x, np.float32).astype(ml_dtypes.bfloat16).astype(np.float64), axis, -1)
    blocks = v.reshape(v.shape[:-1] + (-1, 32))
    amax = np.abs(blocks).max(-1, keepdims=True)
    byte = np.maximum(np.where(amax > 0, np.frexp(amax)[1] - 1 + 127, 0) - down, 1)
    scale = np.exp2(byte - 127.0)
    codes = (blocks / scale).astype(np.float32).astype(dtype).astype(np.float64)
    return np.moveaxis((codes * scale).reshape(v.shape), -1, axis)


WIDE = False


def mx_kscale(k):
    if not WIDE:
        return np.ones(k)
    levels = np.array([10, -10, 5, -5, 0])
    a = np.random.permutation(np.resize(levels, k // 512 * 4)).reshape(k // 512, 4)
    idx = np.arange(k)
    return np.exp2(a[idx // 512, idx % 128 // 32])


BF16 = ml_dtypes.bfloat16


def bf(x):
    return np.asarray(x, np.float32).astype(BF16)


def f64(x):
    return np.asarray(x).astype(np.float64)


E2M1 = np.array([0.0, 0.5, 1.0, 1.5, 2.0, 3.0, 4.0, 6.0, -0.0, -0.5, -1.0, -1.5, -2.0, -3.0, -4.0, -6.0])


def pack_weight(w, fmt):
    k, n = w.shape
    w = f64(bf(w)).reshape(k // 32, 32, n)
    amax = np.abs(w).max(1)
    if fmt == "e4m3":
        byte = np.frexp(amax)[1] - 1 + 127 - 7
    else:
        mant, ex = np.frexp(amax / 6.0)
        byte = np.where(mant > 0.5, ex, ex - 1) + 127
    byte = np.clip(np.where(amax > 0, byte, 1), 1, 254)
    scaled = (w * np.exp2(127.0 - byte)[:, None, :]).reshape(k, n).astype(np.float32)
    by_word = np.ascontiguousarray(scaled.reshape(k // 512, 128, 4, n).transpose(0, 1, 3, 2))
    if fmt == "e4m3":
        words = by_word.astype(ml_dtypes.float8_e4m3fn).view(np.uint8)
    else:
        c = by_word.astype(ml_dtypes.float4_e2m1fn).view(np.uint8) & 0xF
        words = c[..., 0::2] | (c[..., 1::2] << 4)
    return np.ascontiguousarray(words), np.ascontiguousarray(byte.astype(np.uint8).reshape(k // 512, 16, n))


def unpack_weight(words, scales, fmt):
    g, p, n, _ = words.shape
    if fmt == "e4m3":
        vals = np.ascontiguousarray(words).view(ml_dtypes.float8_e4m3fn).astype(np.float64)
    else:
        nib = np.empty((g, p, n, 4), np.uint8)
        nib[..., 0::2] = words & 0xF
        nib[..., 1::2] = words >> 4
        vals = E2M1[nib]
    vals = vals * np.repeat(np.exp2(scales.astype(np.float64) - 127.0), 8, axis=1)[..., None]
    return vals.transpose(0, 1, 3, 2).reshape(g * 512, n)

def pack4(w):
    words, scales = pack_weight(w, "e2m1")
    return words.reshape(words.shape[0], 128, -1), scales


def unpack4(words, scales):
    return unpack_weight(words.reshape(words.shape[0], 128, -1, 2), scales, "e2m1")


N, P, D, E, F = 128, 3, 16384, 256, 1024


def setup_inputs():
    s = mx_kscale(D)
    x = np.random.standard_normal((N, P, D)) + 0.5 * np.random.standard_normal((1, P, D))
    w1a_words, w1a_scales = pack4(np.random.standard_normal((D, E)) / np.sqrt(D) / s[:, None])
    w2a_words, w2a_scales = pack4(np.random.standard_normal((D, E)) / np.sqrt(D) / s[:, None])
    return {"x": bf(x * s),
            "w1a_words": w1a_words, "w1a_scales": w1a_scales,
            "w2a_words": w2a_words, "w2a_scales": w2a_scales}


def reference(x, w1a_words, w1a_scales, w2a_words, w2a_scales):
    h = f64(x)
    neigh = (h.sum(axis=1, keepdims=True) - h) * 0.5
    return (mxq(h, 2, "e4m3") @ unpack4(w2a_words, w2a_scales)) + (mxq(neigh, 2, "e4m3") @ unpack4(w1a_words, w1a_scales))

@@ -1,0 +1,210 @@
+from contextlib import ExitStack
+
+import concourse.mybir as mybir
+from concourse.masks import make_identity
+
+F32 = mybir.dt.float32
+BF16 = mybir.dt.bfloat16
+I32 = mybir.dt.int32
+U32 = mybir.dt.uint32
+U8 = mybir.dt.uint8
+FP8X4 = mybir.dt.float8_e4m3fn_x4
+FP4X4 = mybir.dt.float4_e2m1fn_x4
+ADD = mybir.AluOpType.add
+MULT = mybir.AluOpType.mult
+
+P = 128
+ITEMS, HOPS, D, E = 128, 3, 16384, 256
+PACK = 4
+K_PASS = P * PACK
+PASSES = D // K_PASS
+WORDS_PASS = K_PASS // 2
+COLS_PASS = HOPS * ITEMS
+N_MOVING = 512
+PAD = N_MOVING - COLS_PASS
+E_TILE = 128
+E_TILES = E // E_TILE
+
+ROUND_PASSES = 2
+ROUNDS = PASSES // ROUND_PASSES
+ROUND_COLS = ROUND_PASSES * COLS_PASS
+CHUNK_ROUNDS = 2
+CHUNK_K = CHUNK_ROUNDS * ROUND_PASSES * K_PASS
+CHUNKS = D // CHUNK_K
+X_BUFS = 4
+GROUP_PASSES = 8
+GROUPS = PASSES // GROUP_PASSES
+CODE_BUFS = 3
+
+FLOPS = 2 * 2 * ITEMS * HOPS * D * E
+
+
+def tile_dogtaitujuanji_pa_k_kernel(
+    tc, x, w1a_words, w1a_scales, w2a_words, w2a_scales, out
+):
+    nc = tc.nc
+    dram_words = (w2a_words, w1a_words)
+    dram_scales = (w2a_scales, w1a_scales)
+
+    with ExitStack() as ctx:
+        keep = ctx.enter_context(tc.tile_pool(name="keep", bufs=1))
+        raw_pool = ctx.enter_context(tc.tile_pool(name="raw", bufs=X_BUFS))
+        grouped_pool = ctx.enter_context(tc.tile_pool(name="grouped", bufs=3))
+        end_pool = ctx.enter_context(tc.tile_pool(name="end", bufs=2))
+        acc_pool = ctx.enter_context(tc.psum_pool(name="acc", bufs=1))
+        turn_pool = ctx.enter_context(tc.psum_pool(name="turn", bufs=4))
+
+        identity = keep.tile([P, P], F32, name="identity")
+        make_identity(nc, identity[:])
+
+        w_words = keep.tile([P, PASSES, 2, 2 * E], U8, name="w_words", align_bytes=64)
+        w_planes = keep.tile([P, PASSES, 2, E], U8, name="w_planes", align_bytes=64)
+        for j in range(GROUPS):
+            group = slice(j * GROUP_PASSES, (j + 1) * GROUP_PASSES)
+            nc.vector.memset(w_planes[:, group].bitcast(I32), 0)
+
+        codes = [
+            [
+                keep.tile([P, ROUND_COLS + PAD], U32, name="codes%d_%d" % (o, b), align_bytes=64)
+                for b in range(CODE_BUFS)
+            ]
+            for o in range(2)
+        ]
+        planes = [
+            [
+                keep.tile([P, ROUND_COLS + PAD], U8, name="planes%d_%d" % (o, b), align_bytes=64)
+                for b in range(CODE_BUFS)
+            ]
+            for o in range(2)
+        ]
+        for o in range(2):
+            for b in range(CODE_BUFS):
+                nc.vector.memset(codes[o][b][:, ROUND_COLS:].bitcast(I32), 0)
+                nc.vector.memset(planes[o][b][:, ROUND_COLS:].bitcast(I32), 0)
+
+        acc = [
+            [acc_pool.tile([E_TILE, N_MOVING], F32, name="acc%d_%d" % (o, h)) for h in range(E_TILES)]
+            for o in range(2)
+        ]
+
+        def load_weights(j):
+            group = slice(j * GROUP_PASSES, (j + 1) * GROUP_PASSES)
+            for o in range(2):
+                for r in range(4):
+                    nc.sync.dma_start(
+                        out=w_planes[r:P:32, group, o, :].bitcast(I32),
+                        in_=dram_scales[o][group, r:16:4, :].bitcast(I32).rearrange("g q n -> q g n"),
+                    )
+            for o in range(2):
+                nc.sync.dma_start(
+                    out=w_words[:, group, o, :].bitcast(I32),
+                    in_=dram_words[o][group].bitcast(I32).rearrange("g j b -> j g b"),
+                )
+
+        raw = {}
+
+        def load_x(c):
+            raw[c] = raw_pool.tile([P, HOPS, CHUNK_K], BF16, name="raw")
+            nc.sync.dma_start(out=raw[c][:], in_=x[:, :, c * CHUNK_K : (c + 1) * CHUNK_K])
+
+        grouped = {}
+
+        def turn(r):
+            words = raw[r // CHUNK_ROUNDS][:].bitcast(F32)
+            first = (r % CHUNK_ROUNDS) * ROUND_PASSES * WORDS_PASS
+            x_grouped = grouped_pool.tile(
+                [P, ROUND_PASSES, HOPS, ITEMS, PACK], BF16, name="x_grouped", align_bytes=64
+            )
+            for p in range(HOPS):
+                turned = turn_pool.tile([P, ROUND_PASSES, 2, ITEMS], F32, name="turned")
+                for g in range(ROUND_PASSES):
+                    for u in range(2):
+                        start = first + g * WORDS_PASS
+                        nc.tensor.transpose(
+                            turned[:, g, u, :],
+                            words[:, p, start + u : start + WORDS_PASS : 2],
+                            identity[:],
+                        )
+                nc.scalar.copy(
+                    out=x_grouped[:].bitcast(F32)[:, :, p, :, :],
+                    in_=turned[:].rearrange("j g u n -> j g n u"),
+                )
+            grouped[r] = x_grouped
+
+        def quantise(values, o, b):
+            flat = values[:].rearrange("j g p n t -> j (g p n t)")
+            for lo, hi in ((0, 512), (512, ROUND_COLS)):
+                nc.vector.quantize_mx(
+                    out=codes[o][b][:, lo:hi].bitcast(FP8X4),
+                    scales=planes[o][b][:, lo:hi],
+                    in_=flat[:, PACK * lo : PACK * hi],
+                )
+
+        def prepare(r):
+            x_grouped = grouped[r]
+            pair_grouped = grouped_pool.tile(
+                [P, ROUND_PASSES, HOPS, ITEMS, PACK], BF16, name="pair_grouped", align_bytes=64
+            )
+            for p in range(HOPS):
+                nc.vector.tensor_tensor(
+                    out=pair_grouped[:, :, p],
+                    in0=x_grouped[:, :, (p + 1) % HOPS],
+                    in1=x_grouped[:, :, (p + 2) % HOPS],
+                    op=ADD,
+                )
+            quantise(x_grouped, 0, r % CODE_BUFS)
+            quantise(pair_grouped, 1, r % CODE_BUFS)
+
+        def multiply(r):
+            b = r % CODE_BUFS
+            for o in range(2):
+                for g in range(ROUND_PASSES):
+                    k_pass = r * ROUND_PASSES + g
+                    window = slice(g * COLS_PASS, g * COLS_PASS + N_MOVING)
+                    for h in range(E_TILES):
+                        nc.tensor.matmul_mx(
+                            out=acc[o][h][:],
+                            lhsT=w_words[:, k_pass, o, 2 * E_TILE * h : 2 * E_TILE * (h + 1)].bitcast(FP4X4),
+                            lhsT_scale=w_planes[:, k_pass, o, E_TILE * h : E_TILE * (h + 1)],
+                            rhs=codes[o][b][:, window].bitcast(FP8X4),
+                            rhs_scale=planes[o][b][:, window],
+                            start=(k_pass == 0),
+                            stop=(k_pass == PASSES - 1),
+                        )
+
+        load_x(0)
+        load_weights(0)
+        for c in range(1, X_BUFS - 1):
+            load_x(c)
+        for r in range(ROUNDS + 2):
+            if r % CHUNK_ROUNDS == 0:
+                c = r // CHUNK_ROUNDS
+                if c + X_BUFS - 1 < CHUNKS:
+                    load_x(c + X_BUFS - 1)
+                if c % 2 == 1 and (c + 1) // 2 < GROUPS:
+                    load_weights((c + 1) // 2)
+            if r < ROUNDS:
+                turn(r)
+            if 0 <= r - 1 < ROUNDS:
+                prepare(r - 1)
+            if 0 <= r - 2:
+                multiply(r - 2)
+
+        total = []
+        for h in range(E_TILES):
+            own = end_pool.tile([E_TILE, COLS_PASS], F32, name="own")
+            nc.scalar.copy(out=own[:], in_=acc[0][h][:, 0:COLS_PASS])
+            summed = end_pool.tile([E_TILE, COLS_PASS], F32, name="summed")
+            nc.vector.scalar_tensor_tensor(
+                out=summed[:], in0=acc[1][h][:, 0:COLS_PASS], scalar=0.5, in1=own[:], op0=MULT, op1=ADD
+            )
+            total.append(summed)
+        out_rows = keep.tile([ITEMS, HOPS, E], F32, name="out_rows")
+        for p in range(HOPS):
+            back = turn_pool.tile([ITEMS, E_TILES, E_TILE], F32, name="back", tag="turned")
+            for h in range(E_TILES):
+                nc.tensor.transpose(
+                    back[:, h, :], total[h][:, p * ITEMS : (p + 1) * ITEMS], identity[:]
+                )
+            nc.scalar.copy(out=out_rows[:, p, :], in_=back[:].rearrange("n h e -> n (h e)"))
+        nc.sync.dma_start(out=out[:, :, :], in_=out_rows[:])

@@ -49,6 +49,7 @@ def tile_dogtaitujuanji_pa_k_kernel(
     with ExitStack() as ctx:
         keep = ctx.enter_context(tc.tile_pool(name="keep", bufs=1))
         raw_pool = ctx.enter_context(tc.tile_pool(name="raw", bufs=X_BUFS))
+        sorted_pool = ctx.enter_context(tc.tile_pool(name="sorted", bufs=6))
         grouped_pool = ctx.enter_context(tc.tile_pool(name="grouped", bufs=3))
         end_pool = ctx.enter_context(tc.tile_pool(name="end", bufs=2))
         acc_pool = ctx.enter_context(tc.psum_pool(name="acc", bufs=1))
@@ -107,11 +108,23 @@ def tile_dogtaitujuanji_pa_k_kernel(
             raw[c] = raw_pool.tile([P, HOPS, CHUNK_K], BF16, name="raw")
             nc.sync.dma_start(out=raw[c][:], in_=x[:, :, c * CHUNK_K : (c + 1) * CHUNK_K])
 
+        sorted_words = {}
+
+        def sort(r):
+            words = raw[r // CHUNK_ROUNDS][:].bitcast(F32)
+            first = (r % CHUNK_ROUNDS) * ROUND_PASSES * WORDS_PASS
+            for p in range(HOPS):
+                sorted_words[r, p] = sorted_pool.tile([P, ROUND_PASSES, 2, P], F32, name="sorted_words")
+                nc.scalar.copy(
+                    out=sorted_words[r, p][:],
+                    in_=words[:, p, first : first + ROUND_PASSES * WORDS_PASS].rearrange(
+                        "n (g j u) -> n g u j", g=ROUND_PASSES, u=2
+                    ),
+                )
+
         grouped = {}
 
         def turn(r):
-            words = raw[r // CHUNK_ROUNDS][:].bitcast(F32)
-            first = (r % CHUNK_ROUNDS) * ROUND_PASSES * WORDS_PASS
             x_grouped = grouped_pool.tile(
                 [P, ROUND_PASSES, HOPS, ITEMS, PACK], BF16, name="x_grouped", align_bytes=64
             )
@@ -119,12 +132,7 @@ def tile_dogtaitujuanji_pa_k_kernel(
                 turned = turn_pool.tile([P, ROUND_PASSES, 2, ITEMS], F32, name="turned")
                 for g in range(ROUND_PASSES):
                     for u in range(2):
-                        start = first + g * WORDS_PASS
-                        nc.tensor.transpose(
-                            turned[:, g, u, :],
-                            words[:, p, start + u : start + WORDS_PASS : 2],
-                            identity[:],
-                        )
+                        nc.tensor.transpose(turned[:, g, u, :], sorted_words[r, p][:, g, u, :], identity[:])
                 nc.scalar.copy(
                     out=x_grouped[:].bitcast(F32)[:, :, p, :, :],
                     in_=turned[:].rearrange("j g u n -> j g n u"),
@@ -176,6 +184,7 @@ def tile_dogtaitujuanji_pa_k_kernel(
         load_weights(0)
         for c in range(1, X_BUFS - 1):
             load_x(c)
+        sort(0)
         for r in range(ROUNDS + 2):
             if r % CHUNK_ROUNDS == 0:
                 c = r // CHUNK_ROUNDS
@@ -183,6 +192,8 @@ def tile_dogtaitujuanji_pa_k_kernel(
                     load_x(c + X_BUFS - 1)
                 if c % 2 == 1 and (c + 1) // 2 < GROUPS:
                     load_weights((c + 1) // 2)
+            if r + 1 < ROUNDS:
+                sort(r + 1)
             if r < ROUNDS:
                 turn(r)
             if 0 <= r - 1 < ROUNDS:

@@ -49,11 +49,11 @@ def tile_dogtaitujuanji_pa_k_kernel(
     with ExitStack() as ctx:
         keep = ctx.enter_context(tc.tile_pool(name="keep", bufs=1))
         raw_pool = ctx.enter_context(tc.tile_pool(name="raw", bufs=X_BUFS))
-        sorted_pool = ctx.enter_context(tc.tile_pool(name="sorted", bufs=6))
         grouped_pool = ctx.enter_context(tc.tile_pool(name="grouped", bufs=3))
         end_pool = ctx.enter_context(tc.tile_pool(name="end", bufs=2))
         acc_pool = ctx.enter_context(tc.psum_pool(name="acc", bufs=1))
         turn_pool = ctx.enter_context(tc.psum_pool(name="turn", bufs=4))
+        ctx.enter_context(tc.manual_schedule())
 
         identity = keep.tile([P, P], F32, name="identity")
         make_identity(nc, identity[:])
@@ -108,23 +108,11 @@ def tile_dogtaitujuanji_pa_k_kernel(
             raw[c] = raw_pool.tile([P, HOPS, CHUNK_K], BF16, name="raw")
             nc.sync.dma_start(out=raw[c][:], in_=x[:, :, c * CHUNK_K : (c + 1) * CHUNK_K])
 
-        sorted_words = {}
-
-        def sort(r):
-            words = raw[r // CHUNK_ROUNDS][:].bitcast(F32)
-            first = (r % CHUNK_ROUNDS) * ROUND_PASSES * WORDS_PASS
-            for p in range(HOPS):
-                sorted_words[r, p] = sorted_pool.tile([P, ROUND_PASSES, 2, P], F32, name="sorted_words")
-                nc.scalar.copy(
-                    out=sorted_words[r, p][:],
-                    in_=words[:, p, first : first + ROUND_PASSES * WORDS_PASS].rearrange(
-                        "n (g j u) -> n g u j", g=ROUND_PASSES, u=2
-                    ),
-                )
-
         grouped = {}
 
         def turn(r):
+            words = raw[r // CHUNK_ROUNDS][:].bitcast(F32)
+            first = (r % CHUNK_ROUNDS) * ROUND_PASSES * WORDS_PASS
             x_grouped = grouped_pool.tile(
                 [P, ROUND_PASSES, HOPS, ITEMS, PACK], BF16, name="x_grouped", align_bytes=64
             )
@@ -132,7 +120,12 @@ def tile_dogtaitujuanji_pa_k_kernel(
                 turned = turn_pool.tile([P, ROUND_PASSES, 2, ITEMS], F32, name="turned")
                 for g in range(ROUND_PASSES):
                     for u in range(2):
-                        nc.tensor.transpose(turned[:, g, u, :], sorted_words[r, p][:, g, u, :], identity[:])
+                        start = first + g * WORDS_PASS
+                        nc.tensor.transpose(
+                            turned[:, g, u, :],
+                            words[:, p, start + u : start + WORDS_PASS : 2],
+                            identity[:],
+                        )
                 nc.scalar.copy(
                     out=x_grouped[:].bitcast(F32)[:, :, p, :, :],
                     in_=turned[:].rearrange("j g u n -> j g n u"),
@@ -184,7 +177,6 @@ def tile_dogtaitujuanji_pa_k_kernel(
         load_weights(0)
         for c in range(1, X_BUFS - 1):
             load_x(c)
-        sort(0)
         for r in range(ROUNDS + 2):
             if r % CHUNK_ROUNDS == 0:
                 c = r // CHUNK_ROUNDS
@@ -192,8 +184,6 @@ def tile_dogtaitujuanji_pa_k_kernel(
                     load_x(c + X_BUFS - 1)
                 if c % 2 == 1 and (c + 1) // 2 < GROUPS:
                     load_weights((c + 1) // 2)
-            if r + 1 < ROUNDS:
-                sort(r + 1)
             if r < ROUNDS:
                 turn(r)
             if 0 <= r - 1 < ROUNDS:

@@ -25,14 +25,16 @@ PAD = N_MOVING - COLS_PASS
 E_TILE = 128
 E_TILES = E // E_TILE
 
-ROUND_PASSES = 2
+UNIT_PASSES = 2
+UNIT_K = UNIT_PASSES * K_PASS
+UNITS = PASSES // UNIT_PASSES
+ROUND_UNITS = 2
+ROUND_PASSES = ROUND_UNITS * UNIT_PASSES
 ROUNDS = PASSES // ROUND_PASSES
 ROUND_COLS = ROUND_PASSES * COLS_PASS
-CHUNK_ROUNDS = 2
-CHUNK_K = CHUNK_ROUNDS * ROUND_PASSES * K_PASS
-CHUNKS = D // CHUNK_K
-X_BUFS = 4
+X_BUFS = 6
 GROUP_PASSES = 8
+GROUP_ROUNDS = GROUP_PASSES // ROUND_PASSES
 GROUPS = PASSES // GROUP_PASSES
 CODE_BUFS = 3
 
@@ -50,6 +52,7 @@ def tile_dogtaitujuanji_pa_k_kernel(
         keep = ctx.enter_context(tc.tile_pool(name="keep", bufs=1))
         raw_pool = ctx.enter_context(tc.tile_pool(name="raw", bufs=X_BUFS))
         grouped_pool = ctx.enter_context(tc.tile_pool(name="grouped", bufs=3))
+        pair_pool = ctx.enter_context(tc.tile_pool(name="pair", bufs=2))
         end_pool = ctx.enter_context(tc.tile_pool(name="end", bufs=2))
         acc_pool = ctx.enter_context(tc.psum_pool(name="acc", bufs=1))
         turn_pool = ctx.enter_context(tc.psum_pool(name="turn", bufs=4))
@@ -104,37 +107,38 @@ def tile_dogtaitujuanji_pa_k_kernel(
 
         raw = {}
 
-        def load_x(c):
-            raw[c] = raw_pool.tile([P, HOPS, CHUNK_K], BF16, name="raw")
-            nc.sync.dma_start(out=raw[c][:], in_=x[:, :, c * CHUNK_K : (c + 1) * CHUNK_K])
+        def load_x(i):
+            raw[i] = raw_pool.tile([P, HOPS, UNIT_K], BF16, name="raw")
+            nc.sync.dma_start(out=raw[i][:], in_=x[:, :, i * UNIT_K : (i + 1) * UNIT_K])
 
         grouped = {}
 
-        def turn(r):
-            words = raw[r // CHUNK_ROUNDS][:].bitcast(F32)
-            first = (r % CHUNK_ROUNDS) * ROUND_PASSES * WORDS_PASS
-            x_grouped = grouped_pool.tile(
-                [P, ROUND_PASSES, HOPS, ITEMS, PACK], BF16, name="x_grouped", align_bytes=64
-            )
+        def turn(i):
+            r = i // ROUND_UNITS
+            if i % ROUND_UNITS == 0:
+                grouped[r] = grouped_pool.tile(
+                    [P, ROUND_PASSES, HOPS, ITEMS, PACK], BF16, name="x_grouped", align_bytes=64
+                )
+            first = (i % ROUND_UNITS) * UNIT_PASSES
+            unit_grouped = grouped[r][:, first : first + UNIT_PASSES].bitcast(F32)
+            words = raw[i][:].bitcast(F32)
             for p in range(HOPS):
-                turned = turn_pool.tile([P, ROUND_PASSES, 2, ITEMS], F32, name="turned")
-                for g in range(ROUND_PASSES):
+                turned = turn_pool.tile([P, UNIT_PASSES, 2, ITEMS], F32, name="turned")
+                for g in range(UNIT_PASSES):
                     for u in range(2):
-                        start = first + g * WORDS_PASS
                         nc.tensor.transpose(
                             turned[:, g, u, :],
-                            words[:, p, start + u : start + WORDS_PASS : 2],
+                            words[:, p, g * WORDS_PASS + u : (g + 1) * WORDS_PASS : 2],
                             identity[:],
                         )
                 nc.scalar.copy(
-                    out=x_grouped[:].bitcast(F32)[:, :, p, :, :],
+                    out=unit_grouped[:, :, p, :, :],
                     in_=turned[:].rearrange("j g u n -> j g n u"),
                 )
-            grouped[r] = x_grouped
 
         def quantise(values, o, b):
             flat = values[:].rearrange("j g p n t -> j (g p n t)")
-            for lo, hi in ((0, 512), (512, ROUND_COLS)):
+            for lo, hi in ((0, 1024), (1024, ROUND_COLS)):
                 nc.vector.quantize_mx(
                     out=codes[o][b][:, lo:hi].bitcast(FP8X4),
                     scales=planes[o][b][:, lo:hi],
@@ -143,7 +147,7 @@ def tile_dogtaitujuanji_pa_k_kernel(
 
         def prepare(r):
             x_grouped = grouped[r]
-            pair_grouped = grouped_pool.tile(
+            pair_grouped = pair_pool.tile(
                 [P, ROUND_PASSES, HOPS, ITEMS, PACK], BF16, name="pair_grouped", align_bytes=64
             )
             for p in range(HOPS):
@@ -156,40 +160,40 @@ def tile_dogtaitujuanji_pa_k_kernel(
             quantise(x_grouped, 0, r % CODE_BUFS)
             quantise(pair_grouped, 1, r % CODE_BUFS)
 
-        def multiply(r):
+        def multiply(r, o):
             b = r % CODE_BUFS
-            for o in range(2):
-                for g in range(ROUND_PASSES):
-                    k_pass = r * ROUND_PASSES + g
-                    window = slice(g * COLS_PASS, g * COLS_PASS + N_MOVING)
-                    for h in range(E_TILES):
-                        nc.tensor.matmul_mx(
-                            out=acc[o][h][:],
-                            lhsT=w_words[:, k_pass, o, 2 * E_TILE * h : 2 * E_TILE * (h + 1)].bitcast(FP4X4),
-                            lhsT_scale=w_planes[:, k_pass, o, E_TILE * h : E_TILE * (h + 1)],
-                            rhs=codes[o][b][:, window].bitcast(FP8X4),
-                            rhs_scale=planes[o][b][:, window],
-                            start=(k_pass == 0),
-                            stop=(k_pass == PASSES - 1),
-                        )
+            for g in range(ROUND_PASSES):
+                k_pass = r * ROUND_PASSES + g
+                window = slice(g * COLS_PASS, g * COLS_PASS + N_MOVING)
+                for h in range(E_TILES):
+                    nc.tensor.matmul_mx(
+                        out=acc[o][h][:],
+                        lhsT=w_words[:, k_pass, o, 2 * E_TILE * h : 2 * E_TILE * (h + 1)].bitcast(FP4X4),
+                        lhsT_scale=w_planes[:, k_pass, o, E_TILE * h : E_TILE * (h + 1)],
+                        rhs=codes[o][b][:, window].bitcast(FP8X4),
+                        rhs_scale=planes[o][b][:, window],
+                        start=(k_pass == 0),
+                        stop=(k_pass == PASSES - 1),
+                    )
 
         load_x(0)
+        load_x(1)
         load_weights(0)
-        for c in range(1, X_BUFS - 1):
-            load_x(c)
+        for i in range(2, X_BUFS - 1):
+            load_x(i)
         for r in range(ROUNDS + 2):
-            if r % CHUNK_ROUNDS == 0:
-                c = r // CHUNK_ROUNDS
-                if c + X_BUFS - 1 < CHUNKS:
-                    load_x(c + X_BUFS - 1)
-                if c % 2 == 1 and (c + 1) // 2 < GROUPS:
-                    load_weights((c + 1) // 2)
-            if r < ROUNDS:
-                turn(r)
-            if 0 <= r - 1 < ROUNDS:
-                prepare(r - 1)
-            if 0 <= r - 2:
-                multiply(r - 2)
+            if r % GROUP_ROUNDS == 0 and 0 < r // GROUP_ROUNDS < GROUPS:
+                load_weights(r // GROUP_ROUNDS)
+            for half in range(ROUND_UNITS):
+                i = r * ROUND_UNITS + half
+                if i + X_BUFS - 1 < UNITS:
+                    load_x(i + X_BUFS - 1)
+                if i < UNITS:
+                    turn(i)
+                if half == 0 and 0 <= r - 1 < ROUNDS:
+                    prepare(r - 1)
+                if 0 <= r - 2:
+                    multiply(r - 2, half)
 
         total = []
         for h in range(E_TILES):

@@ -19,24 +19,15 @@ PACK = 4
 K_PASS = P * PACK
 PASSES = D // K_PASS
 WORDS_PASS = K_PASS // 2
-COLS_PASS = HOPS * ITEMS
-N_MOVING = 512
-PAD = N_MOVING - COLS_PASS
-E_TILE = 128
-E_TILES = E // E_TILE
+N_MOVING = 128
 
-UNIT_PASSES = 2
-UNIT_K = UNIT_PASSES * K_PASS
-UNITS = PASSES // UNIT_PASSES
-ROUND_UNITS = 2
-ROUND_PASSES = ROUND_UNITS * UNIT_PASSES
-ROUNDS = PASSES // ROUND_PASSES
-ROUND_COLS = ROUND_PASSES * COLS_PASS
-X_BUFS = 6
-GROUP_PASSES = 8
-GROUP_ROUNDS = GROUP_PASSES // ROUND_PASSES
-GROUPS = PASSES // GROUP_PASSES
-CODE_BUFS = 3
+ROUND_PASSES = (1, 1) + (2,) * 14 + (1, 1)
+ROUNDS = len(ROUND_PASSES)
+ROUND_START = [sum(ROUND_PASSES[:r]) for r in range(ROUNDS)]
+X_BUFS = 8
+SORTED_HOPS = 0
+SORT_FROM = 2
+LAG = 2
 
 FLOPS = 2 * 2 * ITEMS * HOPS * D * E
 
@@ -51,165 +42,181 @@ def tile_dogtaitujuanji_pa_k_kernel(
     with ExitStack() as ctx:
         keep = ctx.enter_context(tc.tile_pool(name="keep", bufs=1))
         raw_pool = ctx.enter_context(tc.tile_pool(name="raw", bufs=X_BUFS))
+        sorted_pool = ctx.enter_context(tc.tile_pool(name="sorted", bufs=3))
         grouped_pool = ctx.enter_context(tc.tile_pool(name="grouped", bufs=3))
         pair_pool = ctx.enter_context(tc.tile_pool(name="pair", bufs=2))
-        end_pool = ctx.enter_context(tc.tile_pool(name="end", bufs=2))
+        code_pool = ctx.enter_context(tc.tile_pool(name="codes", bufs=4))
+        end_pool = ctx.enter_context(tc.tile_pool(name="end", bufs=3))
         acc_pool = ctx.enter_context(tc.psum_pool(name="acc", bufs=1))
-        turn_pool = ctx.enter_context(tc.psum_pool(name="turn", bufs=4))
+        turn_pool = ctx.enter_context(tc.psum_pool(name="turn", bufs=5))
         ctx.enter_context(tc.manual_schedule())
 
         identity = keep.tile([P, P], F32, name="identity")
         make_identity(nc, identity[:])
 
-        w_words = keep.tile([P, PASSES, 2, 2 * E], U8, name="w_words", align_bytes=64)
-        w_planes = keep.tile([P, PASSES, 2, E], U8, name="w_planes", align_bytes=64)
-        for j in range(GROUPS):
-            group = slice(j * GROUP_PASSES, (j + 1) * GROUP_PASSES)
-            nc.vector.memset(w_planes[:, group].bitcast(I32), 0)
+        w_words = keep.tile([P, 1 + 2 * PASSES, 2 * E], U8, name="w_words", align_bytes=64)
+        w_planes = keep.tile([P, 1 + 2 * PASSES, E], U8, name="w_planes", align_bytes=64)
+        words_view = w_words[:, 1:, :].rearrange("j (g o) b -> j g o b", o=2)
+        planes_view = w_planes[:, 1:, :].rearrange("j (g o) n -> j g o n", o=2)
+        nc.vector.memset(w_words[:, 0, :].bitcast(I32), 0)
+        for lo, hi in ((0, 9), (9, 37), (37, 65)):
+            nc.vector.memset(w_planes[:, lo:hi, :].bitcast(I32), 0)
 
-        codes = [
-            [
-                keep.tile([P, ROUND_COLS + PAD], U32, name="codes%d_%d" % (o, b), align_bytes=64)
-                for b in range(CODE_BUFS)
-            ]
-            for o in range(2)
-        ]
-        planes = [
-            [
-                keep.tile([P, ROUND_COLS + PAD], U8, name="planes%d_%d" % (o, b), align_bytes=64)
-                for b in range(CODE_BUFS)
-            ]
-            for o in range(2)
-        ]
-        for o in range(2):
-            for b in range(CODE_BUFS):
-                nc.vector.memset(codes[o][b][:, ROUND_COLS:].bitcast(I32), 0)
-                nc.vector.memset(planes[o][b][:, ROUND_COLS:].bitcast(I32), 0)
+        acc = [acc_pool.tile([ITEMS, 2 * E], F32, name="acc%d" % p) for p in range(HOPS)]
 
-        acc = [
-            [acc_pool.tile([E_TILE, N_MOVING], F32, name="acc%d_%d" % (o, h)) for h in range(E_TILES)]
-            for o in range(2)
-        ]
-
-        def load_weights(j):
-            group = slice(j * GROUP_PASSES, (j + 1) * GROUP_PASSES)
+        def load_scales(first, count):
+            group = slice(first, first + count)
             for o in range(2):
                 for r in range(4):
                     nc.sync.dma_start(
-                        out=w_planes[r:P:32, group, o, :].bitcast(I32),
+                        out=planes_view[r:P:32, group, o, :].bitcast(I32),
                         in_=dram_scales[o][group, r:16:4, :].bitcast(I32).rearrange("g q n -> q g n"),
                     )
+
+        def load_words(first, count):
+            group = slice(first, first + count)
             for o in range(2):
                 nc.sync.dma_start(
-                    out=w_words[:, group, o, :].bitcast(I32),
+                    out=words_view[:, group, o, :].bitcast(I32),
                     in_=dram_words[o][group].bitcast(I32).rearrange("g j b -> j g b"),
                 )
 
         raw = {}
 
-        def load_x(i):
-            raw[i] = raw_pool.tile([P, HOPS, UNIT_K], BF16, name="raw")
-            nc.sync.dma_start(out=raw[i][:], in_=x[:, :, i * UNIT_K : (i + 1) * UNIT_K])
+        def load_x(r):
+            if r >= ROUNDS:
+                return
+            n = ROUND_PASSES[r]
+            lo = ROUND_START[r] * K_PASS
+            raw[r] = raw_pool.tile([P, HOPS, n * K_PASS], BF16, name="raw")
+            nc.sync.dma_start(out=raw[r][:], in_=x[:, :, lo : lo + n * K_PASS])
+
+        in_order = {}
+
+        def sort(r):
+            if not SORT_FROM <= r < ROUNDS:
+                return
+            n = ROUND_PASSES[r]
+            in_order[r] = sorted_pool.tile([P, SORTED_HOPS, n, 2, P], F32, name="in_order")
+            words = raw[r][:].bitcast(F32)
+            for p in range(SORTED_HOPS):
+                nc.scalar.copy(
+                    out=in_order[r][:, p],
+                    in_=words[:, p].rearrange("i (g j u) -> i g u j", u=2, j=P),
+                )
 
         grouped = {}
 
-        def turn(i):
-            r = i // ROUND_UNITS
-            if i % ROUND_UNITS == 0:
-                grouped[r] = grouped_pool.tile(
-                    [P, ROUND_PASSES, HOPS, ITEMS, PACK], BF16, name="x_grouped", align_bytes=64
-                )
-            first = (i % ROUND_UNITS) * UNIT_PASSES
-            unit_grouped = grouped[r][:, first : first + UNIT_PASSES].bitcast(F32)
-            words = raw[i][:].bitcast(F32)
+        def turn(r):
+            n = ROUND_PASSES[r]
+            grouped[r] = grouped_pool.tile([P, HOPS, n, ITEMS, PACK], BF16, name="x_grouped", align_bytes=64)
+            to = grouped[r][:].bitcast(F32)
+            words = raw[r][:].bitcast(F32)
             for p in range(HOPS):
-                turned = turn_pool.tile([P, UNIT_PASSES, 2, ITEMS], F32, name="turned")
-                for g in range(UNIT_PASSES):
+                turned = turn_pool.tile([P, n, 2, ITEMS], F32, name="turned")
+                for g in range(n):
                     for u in range(2):
-                        nc.tensor.transpose(
-                            turned[:, g, u, :],
-                            words[:, p, g * WORDS_PASS + u : (g + 1) * WORDS_PASS : 2],
-                            identity[:],
-                        )
-                nc.scalar.copy(
-                    out=unit_grouped[:, :, p, :, :],
-                    in_=turned[:].rearrange("j g u n -> j g n u"),
-                )
+                        if p < SORTED_HOPS and r >= SORT_FROM:
+                            source = in_order[r][:, p, g, u, :]
+                        else:
+                            source = words[:, p, g * WORDS_PASS + u : (g + 1) * WORDS_PASS : 2]
+                        nc.tensor.transpose(turned[:, g, u, :], source, identity[:])
+                nc.scalar.copy(out=to[:, p], in_=turned[:].rearrange("j g u n -> j g n u"))
 
-        def quantise(values, o, b):
-            flat = values[:].rearrange("j g p n t -> j (g p n t)")
-            for lo, hi in ((0, 1024), (1024, ROUND_COLS)):
-                nc.vector.quantize_mx(
-                    out=codes[o][b][:, lo:hi].bitcast(FP8X4),
-                    scales=planes[o][b][:, lo:hi],
-                    in_=flat[:, PACK * lo : PACK * hi],
-                )
+        codes = {}
+
+        def quantise(flat, r, o, lo, hi):
+            c, s = codes[r, o]
+            nc.vector.quantize_mx(
+                out=c[:, lo:hi].bitcast(FP8X4), scales=s[:, lo:hi], in_=flat[:, PACK * lo : PACK * hi]
+            )
 
         def prepare(r):
-            x_grouped = grouped[r]
-            pair_grouped = pair_pool.tile(
-                [P, ROUND_PASSES, HOPS, ITEMS, PACK], BF16, name="pair_grouped", align_bytes=64
+            n = ROUND_PASSES[r]
+            hop = n * ITEMS
+            pair = pair_pool.tile([P, HOPS * hop * PACK], BF16, name="pair", align_bytes=64)
+            for o in range(2):
+                c = code_pool.tile([P, HOPS * hop], U32, name="codes%d" % o, align_bytes=64)
+                s = code_pool.tile([P, HOPS * hop], U8, name="planes%d" % o, align_bytes=64)
+                codes[r, o] = (c, s)
+            own = grouped[r][:].rearrange("j p g n t -> j (p g n t)")
+            w = hop * PACK
+            quantise(own, r, 0, 0, 2 * hop)
+            nc.vector.tensor_tensor(
+                out=pair[:, 0 : 2 * w], in0=own[:, 0 : 2 * w], in1=own[:, w : 3 * w], op=ADD
             )
-            for p in range(HOPS):
-                nc.vector.tensor_tensor(
-                    out=pair_grouped[:, :, p],
-                    in0=x_grouped[:, :, (p + 1) % HOPS],
-                    in1=x_grouped[:, :, (p + 2) % HOPS],
-                    op=ADD,
-                )
-            quantise(x_grouped, 0, r % CODE_BUFS)
-            quantise(pair_grouped, 1, r % CODE_BUFS)
+            nc.vector.tensor_tensor(
+                out=pair[:, 2 * w :], in0=own[:, 2 * w :], in1=own[:, 0:w], op=ADD
+            )
+            quantise(own, r, 0, 2 * hop, 3 * hop)
+            quantise(pair[:], r, 1, 0, 2 * hop)
+            quantise(pair[:], r, 1, 2 * hop, 3 * hop)
 
         def multiply(r, o):
-            b = r % CODE_BUFS
-            for g in range(ROUND_PASSES):
-                k_pass = r * ROUND_PASSES + g
-                window = slice(g * COLS_PASS, g * COLS_PASS + N_MOVING)
-                for h in range(E_TILES):
-                    nc.tensor.matmul_mx(
-                        out=acc[o][h][:],
-                        lhsT=w_words[:, k_pass, o, 2 * E_TILE * h : 2 * E_TILE * (h + 1)].bitcast(FP4X4),
-                        lhsT_scale=w_planes[:, k_pass, o, E_TILE * h : E_TILE * (h + 1)],
-                        rhs=codes[o][b][:, window].bitcast(FP8X4),
-                        rhs_scale=planes[o][b][:, window],
-                        start=(k_pass == 0),
-                        stop=(k_pass == PASSES - 1),
-                    )
+            n = ROUND_PASSES[r]
+            c, s = codes[r, o]
+            for slot in range(HOPS):
+                p = slot if o == 0 else (slot + 2) % HOPS
+                for g in range(n):
+                    k_pass = ROUND_START[r] + g
+                    lo = (slot * n + g) * ITEMS
+                    own = slice(lo, lo + ITEMS)
+                    w = 1 + 2 * k_pass + o
+                    if k_pass == 0 and o == 0:
+                        nc.tensor.matmul_mx(
+                            out=acc[p][:],
+                            lhsT=c[:, own].bitcast(FP8X4),
+                            lhsT_scale=s[:, own],
+                            rhs=w_words[:, 0:2, :].rearrange("j s b -> j (s b)").bitcast(FP4X4),
+                            rhs_scale=w_planes[:, 0:2, :].rearrange("j s n -> j (s n)"),
+                            start=True,
+                            stop=False,
+                        )
+                        continue
+                    for lo_n in range(0, E, N_MOVING):
+                        at = lo_n + (E if o == 0 else 0)
+                        nc.tensor.matmul_mx(
+                            out=acc[p][:, at : at + N_MOVING],
+                            lhsT=c[:, own].bitcast(FP8X4),
+                            lhsT_scale=s[:, own],
+                            rhs=w_words[:, w, 2 * lo_n : 2 * (lo_n + N_MOVING)].bitcast(FP4X4),
+                            rhs_scale=w_planes[:, w, lo_n : lo_n + N_MOVING],
+                            start=False,
+                            stop=(k_pass == PASSES - 1 and o == 1 and lo_n + N_MOVING == E),
+                        )
 
         load_x(0)
         load_x(1)
-        load_weights(0)
-        for i in range(2, X_BUFS - 1):
-            load_x(i)
-        for r in range(ROUNDS + 2):
-            if r % GROUP_ROUNDS == 0 and 0 < r // GROUP_ROUNDS < GROUPS:
-                load_weights(r // GROUP_ROUNDS)
-            for half in range(ROUND_UNITS):
-                i = r * ROUND_UNITS + half
-                if i + X_BUFS - 1 < UNITS:
-                    load_x(i + X_BUFS - 1)
-                if i < UNITS:
-                    turn(i)
-                if half == 0 and 0 <= r - 1 < ROUNDS:
-                    prepare(r - 1)
-                if 0 <= r - 2:
-                    multiply(r - 2, half)
+        load_x(2)
+        load_scales(0, 4)
+        load_words(0, 4)
+        load_x(3)
+        load_x(4)
+        load_scales(4, 28)
+        load_words(4, 8)
+        load_x(5)
+        load_x(6)
+        for r in range(ROUNDS + LAG):
+            if r == 4:
+                load_words(12, 10)
+            if r == 8:
+                load_words(22, 10)
+            load_x(r + 7)
+            if r < ROUNDS:
+                turn(r)
+            if SORTED_HOPS:
+                sort(r + 1)
+            if 0 <= r - 1 < ROUNDS:
+                prepare(r - 1)
+            if 0 <= r - LAG:
+                multiply(r - LAG, 0)
+                multiply(r - LAG, 1)
 
-        total = []
-        for h in range(E_TILES):
-            own = end_pool.tile([E_TILE, COLS_PASS], F32, name="own")
-            nc.scalar.copy(out=own[:], in_=acc[0][h][:, 0:COLS_PASS])
-            summed = end_pool.tile([E_TILE, COLS_PASS], F32, name="summed")
-            nc.vector.scalar_tensor_tensor(
-                out=summed[:], in0=acc[1][h][:, 0:COLS_PASS], scalar=0.5, in1=own[:], op0=MULT, op1=ADD
-            )
-            total.append(summed)
         out_rows = keep.tile([ITEMS, HOPS, E], F32, name="out_rows")
-        for p in range(HOPS):
-            back = turn_pool.tile([ITEMS, E_TILES, E_TILE], F32, name="back", tag="turned")
-            for h in range(E_TILES):
-                nc.tensor.transpose(
-                    back[:, h, :], total[h][:, p * ITEMS : (p + 1) * ITEMS], identity[:]
-                )
-            nc.scalar.copy(out=out_rows[:, p, :], in_=back[:].rearrange("n h e -> n (h e)"))
-        nc.sync.dma_start(out=out[:, :, :], in_=out_rows[:])
+        for p in (2, 0, 1):
+            own = end_pool.tile([ITEMS, E], F32, name="own")
+            nc.scalar.copy(out=own[:], in_=acc[p][:, E : 2 * E])
+            nc.vector.scalar_tensor_tensor(
+                out=out_rows[:, p, :], in0=acc[p][:, 0:E], scalar=0.5, in1=own[:], op0=MULT, op1=ADD
+            )
+            nc.sync.dma_start(out=out[:, p, :], in_=out_rows[:, p, :])

@@ -28,6 +28,8 @@ X_BUFS = 8
 SORTED_HOPS = 0
 SORT_FROM = 2
 LAG = 2
+WORD_STRETCHES = ((0, 4), (4, 4), (8, 12), (20, 12))
+SCALE_STRETCHES = ((0, 8), (8, 24))
 
 FLOPS = 2 * 2 * ITEMS * HOPS * D * E
 
@@ -54,30 +56,43 @@ def tile_dogtaitujuanji_pa_k_kernel(
         identity = keep.tile([P, P], F32, name="identity")
         make_identity(nc, identity[:])
 
-        w_words = keep.tile([P, 1 + 2 * PASSES, 2 * E], U8, name="w_words", align_bytes=64)
-        w_planes = keep.tile([P, 1 + 2 * PASSES, E], U8, name="w_planes", align_bytes=64)
-        words_view = w_words[:, 1:, :].rearrange("j (g o) b -> j g o b", o=2)
-        planes_view = w_planes[:, 1:, :].rearrange("j (g o) n -> j g o n", o=2)
-        nc.vector.memset(w_words[:, 0, :].bitcast(I32), 0)
-        for lo, hi in ((0, 9), (9, 37), (37, 65)):
-            nc.vector.memset(w_planes[:, lo:hi, :].bitcast(I32), 0)
+        w_words = {}
+        w_planes = {}
+        for j, (first, count) in enumerate(WORD_STRETCHES):
+            lead = 1 if first == 0 else 0
+            w_words[j] = keep.tile([P, lead + 2 * count, 2 * E], U8, name="w_words%d" % j, align_bytes=64)
+            if lead:
+                nc.vector.memset(w_words[j][:, 0, :].bitcast(I32), 0)
+        for j, (first, count) in enumerate(SCALE_STRETCHES):
+            lead = 1 if first == 0 else 0
+            w_planes[j] = keep.tile([P, lead + 2 * count, E], U8, name="w_planes%d" % j, align_bytes=64)
+            nc.vector.memset(w_planes[j][:].bitcast(I32), 0)
+
+        def find(stretches, k_pass, o):
+            for j, (first, count) in enumerate(stretches):
+                if first <= k_pass < first + count:
+                    return j, (1 if first == 0 else 0) + 2 * (k_pass - first) + o
 
         acc = [acc_pool.tile([ITEMS, 2 * E], F32, name="acc%d" % p) for p in range(HOPS)]
 
-        def load_scales(first, count):
+        def load_scales(j):
+            first, count = SCALE_STRETCHES[j]
             group = slice(first, first + count)
+            view = w_planes[j][:, (1 if first == 0 else 0) :, :].rearrange("j (g o) n -> j g o n", o=2)
             for o in range(2):
                 for r in range(4):
                     nc.sync.dma_start(
-                        out=planes_view[r:P:32, group, o, :].bitcast(I32),
+                        out=view[r:P:32, :, o, :].bitcast(I32),
                         in_=dram_scales[o][group, r:16:4, :].bitcast(I32).rearrange("g q n -> q g n"),
                     )
 
-        def load_words(first, count):
+        def load_words(j):
+            first, count = WORD_STRETCHES[j]
             group = slice(first, first + count)
+            view = w_words[j][:, (1 if first == 0 else 0) :, :].rearrange("j (g o) b -> j g o b", o=2)
             for o in range(2):
                 nc.sync.dma_start(
-                    out=words_view[:, group, o, :].bitcast(I32),
+                    out=view[:, :, o, :].bitcast(I32),
                     in_=dram_words[o][group].bitcast(I32).rearrange("g j b -> j g b"),
                 )
 
@@ -161,14 +176,15 @@ def tile_dogtaitujuanji_pa_k_kernel(
                     k_pass = ROUND_START[r] + g
                     lo = (slot * n + g) * ITEMS
                     own = slice(lo, lo + ITEMS)
-                    w = 1 + 2 * k_pass + o
+                    jw, w = find(WORD_STRETCHES, k_pass, o)
+                    jp, q = find(SCALE_STRETCHES, k_pass, o)
                     if k_pass == 0 and o == 0:
                         nc.tensor.matmul_mx(
                             out=acc[p][:],
                             lhsT=c[:, own].bitcast(FP8X4),
                             lhsT_scale=s[:, own],
-                            rhs=w_words[:, 0:2, :].rearrange("j s b -> j (s b)").bitcast(FP4X4),
-                            rhs_scale=w_planes[:, 0:2, :].rearrange("j s n -> j (s n)"),
+                            rhs=w_words[0][:, 0:2, :].rearrange("j s b -> j (s b)").bitcast(FP4X4),
+                            rhs_scale=w_planes[0][:, 0:2, :].rearrange("j s n -> j (s n)"),
                             start=True,
                             stop=False,
                         )
@@ -179,8 +195,8 @@ def tile_dogtaitujuanji_pa_k_kernel(
                             out=acc[p][:, at : at + N_MOVING],
                             lhsT=c[:, own].bitcast(FP8X4),
                             lhsT_scale=s[:, own],
-                            rhs=w_words[:, w, 2 * lo_n : 2 * (lo_n + N_MOVING)].bitcast(FP4X4),
-                            rhs_scale=w_planes[:, w, lo_n : lo_n + N_MOVING],
+                            rhs=w_words[jw][:, w, 2 * lo_n : 2 * (lo_n + N_MOVING)].bitcast(FP4X4),
+                            rhs_scale=w_planes[jp][:, q, lo_n : lo_n + N_MOVING],
                             start=False,
                             stop=(k_pass == PASSES - 1 and o == 1 and lo_n + N_MOVING == E),
                         )
@@ -188,19 +204,18 @@ def tile_dogtaitujuanji_pa_k_kernel(
         load_x(0)
         load_x(1)
         load_x(2)
-        load_scales(0, 4)
-        load_words(0, 4)
+        load_scales(0)
+        load_words(0)
         load_x(3)
         load_x(4)
-        load_scales(4, 28)
-        load_words(4, 8)
+        load_words(1)
         load_x(5)
+        load_scales(1)
         load_x(6)
+        load_words(2)
         for r in range(ROUNDS + LAG):
-            if r == 4:
-                load_words(12, 10)
-            if r == 8:
-                load_words(22, 10)
+            if r == 7:
+                load_words(3)
             load_x(r + 7)
             if r < ROUNDS:
                 turn(r)

@@ -25,10 +25,7 @@ ROUND_PASSES = (1, 1) + (2,) * 14 + (1, 1)
 ROUNDS = len(ROUND_PASSES)
 ROUND_START = [sum(ROUND_PASSES[:r]) for r in range(ROUNDS)]
 X_BUFS = 8
-SORTED_HOPS = 0
-SORT_FROM = 2
-LAG = 2
-WORD_STRETCHES = ((0, 4), (4, 4), (8, 12), (20, 12))
+WORD_STRETCHES = ((0, 2), (2, 2)) + tuple((first, 4) for first in range(4, PASSES, 4))
 SCALE_STRETCHES = ((0, 8), (8, 24))
 
 FLOPS = 2 * 2 * ITEMS * HOPS * D * E
@@ -44,7 +41,6 @@ def tile_dogtaitujuanji_pa_k_kernel(
     with ExitStack() as ctx:
         keep = ctx.enter_context(tc.tile_pool(name="keep", bufs=1))
         raw_pool = ctx.enter_context(tc.tile_pool(name="raw", bufs=X_BUFS))
-        sorted_pool = ctx.enter_context(tc.tile_pool(name="sorted", bufs=3))
         grouped_pool = ctx.enter_context(tc.tile_pool(name="grouped", bufs=3))
         pair_pool = ctx.enter_context(tc.tile_pool(name="pair", bufs=2))
         code_pool = ctx.enter_context(tc.tile_pool(name="codes", bufs=4))
@@ -75,11 +71,11 @@ def tile_dogtaitujuanji_pa_k_kernel(
 
         acc = [acc_pool.tile([ITEMS, 2 * E], F32, name="acc%d" % p) for p in range(HOPS)]
 
-        def load_scales(j):
+        def load_scales(j, operands=(0, 1)):
             first, count = SCALE_STRETCHES[j]
             group = slice(first, first + count)
             view = w_planes[j][:, (1 if first == 0 else 0) :, :].rearrange("j (g o) n -> j g o n", o=2)
-            for o in range(2):
+            for o in operands:
                 for r in range(4):
                     nc.sync.dma_start(
                         out=view[r:P:32, :, o, :].bitcast(I32),
@@ -106,20 +102,6 @@ def tile_dogtaitujuanji_pa_k_kernel(
             raw[r] = raw_pool.tile([P, HOPS, n * K_PASS], BF16, name="raw")
             nc.sync.dma_start(out=raw[r][:], in_=x[:, :, lo : lo + n * K_PASS])
 
-        in_order = {}
-
-        def sort(r):
-            if not SORT_FROM <= r < ROUNDS:
-                return
-            n = ROUND_PASSES[r]
-            in_order[r] = sorted_pool.tile([P, SORTED_HOPS, n, 2, P], F32, name="in_order")
-            words = raw[r][:].bitcast(F32)
-            for p in range(SORTED_HOPS):
-                nc.scalar.copy(
-                    out=in_order[r][:, p],
-                    in_=words[:, p].rearrange("i (g j u) -> i g u j", u=2, j=P),
-                )
-
         grouped = {}
 
         def turn(r):
@@ -131,10 +113,7 @@ def tile_dogtaitujuanji_pa_k_kernel(
                 turned = turn_pool.tile([P, n, 2, ITEMS], F32, name="turned")
                 for g in range(n):
                     for u in range(2):
-                        if p < SORTED_HOPS and r >= SORT_FROM:
-                            source = in_order[r][:, p, g, u, :]
-                        else:
-                            source = words[:, p, g * WORDS_PASS + u : (g + 1) * WORDS_PASS : 2]
+                        source = words[:, p, g * WORDS_PASS + u : (g + 1) * WORDS_PASS : 2]
                         nc.tensor.transpose(turned[:, g, u, :], source, identity[:])
                 nc.scalar.copy(out=to[:, p], in_=turned[:].rearrange("j g u n -> j g n u"))
 
@@ -204,28 +183,29 @@ def tile_dogtaitujuanji_pa_k_kernel(
         load_x(0)
         load_x(1)
         load_x(2)
-        load_scales(0)
-        load_words(0)
         load_x(3)
+        load_words(0)
+        load_scales(0)
         load_x(4)
         load_words(1)
         load_x(5)
-        load_scales(1)
-        load_x(6)
         load_words(2)
-        for r in range(ROUNDS + LAG):
-            if r == 7:
-                load_words(3)
-            load_x(r + 7)
-            if r < ROUNDS:
-                turn(r)
-            if SORTED_HOPS:
-                sort(r + 1)
-            if 0 <= r - 1 < ROUNDS:
-                prepare(r - 1)
-            if 0 <= r - LAG:
-                multiply(r - LAG, 0)
-                multiply(r - LAG, 1)
+        load_scales(1, (0,))
+        load_x(6)
+        load_scales(1, (1,))
+        load_x(7)
+        load_words(3)
+        for step in range(ROUNDS + 2):
+            if step < ROUNDS:
+                turn(step)
+            load_x(step + X_BUFS)
+            if step % 2 == 0 and 4 <= step // 2 + 3 < len(WORD_STRETCHES):
+                load_words(step // 2 + 3)
+            if 0 <= step - 1 < ROUNDS:
+                prepare(step - 1)
+            for r in (0, 1) if step == 3 else (step - 2,) if step > 3 else ():
+                multiply(r, 0)
+                multiply(r, 1)
 
         out_rows = keep.tile([ITEMS, HOPS, E], F32, name="out_rows")
         for p in (2, 0, 1):

from contextlib import ExitStack

import concourse.mybir as mybir
from concourse.masks import make_identity

F32 = mybir.dt.float32
BF16 = mybir.dt.bfloat16
I32 = mybir.dt.int32
U32 = mybir.dt.uint32
U8 = mybir.dt.uint8
FP8X4 = mybir.dt.float8_e4m3fn_x4
FP4X4 = mybir.dt.float4_e2m1fn_x4
ADD = mybir.AluOpType.add
MULT = mybir.AluOpType.mult

P = 128
ITEMS, HOPS, D, E = 128, 3, 16384, 256
PACK = 4
K_PASS = P * PACK
PASSES = D // K_PASS
WORDS_PASS = K_PASS // 2
N_MOVING = 128

ROUND_PASSES = (1, 1) + (2,) * 14 + (1, 1)
ROUNDS = len(ROUND_PASSES)
ROUND_START = [sum(ROUND_PASSES[:r]) for r in range(ROUNDS)]
X_BUFS = 8
WORD_STRETCHES = ((0, 2), (2, 2)) + tuple((first, 4) for first in range(4, PASSES, 4))
SCALE_STRETCHES = ((0, 8), (8, 24))

FLOPS = 2 * 2 * ITEMS * HOPS * D * E


def tile_dogtaitujuanji_pa_k_kernel(
    tc, x, w1a_words, w1a_scales, w2a_words, w2a_scales, out
):
    nc = tc.nc
    dram_words = (w2a_words, w1a_words)
    dram_scales = (w2a_scales, w1a_scales)

    with ExitStack() as ctx:
        keep = ctx.enter_context(tc.tile_pool(name="keep", bufs=1))
        raw_pool = ctx.enter_context(tc.tile_pool(name="raw", bufs=X_BUFS))
        grouped_pool = ctx.enter_context(tc.tile_pool(name="grouped", bufs=3))
        pair_pool = ctx.enter_context(tc.tile_pool(name="pair", bufs=2))
        code_pool = ctx.enter_context(tc.tile_pool(name="codes", bufs=4))
        end_pool = ctx.enter_context(tc.tile_pool(name="end", bufs=3))
        acc_pool = ctx.enter_context(tc.psum_pool(name="acc", bufs=1))
        turn_pool = ctx.enter_context(tc.psum_pool(name="turn", bufs=5))
        ctx.enter_context(tc.manual_schedule())

        identity = keep.tile([P, P], F32, name="identity")
        make_identity(nc, identity[:])

        w_words = {}
        w_planes = {}
        for j, (first, count) in enumerate(WORD_STRETCHES):
            lead = 1 if first == 0 else 0
            w_words[j] = keep.tile([P, lead + 2 * count, 2 * E], U8, name="w_words%d" % j, align_bytes=64)
            if lead:
                nc.vector.memset(w_words[j][:, 0, :].bitcast(I32), 0)
        for j, (first, count) in enumerate(SCALE_STRETCHES):
            lead = 1 if first == 0 else 0
            w_planes[j] = keep.tile([P, lead + 2 * count, E], U8, name="w_planes%d" % j, align_bytes=64)
            nc.vector.memset(w_planes[j][:].bitcast(I32), 0)

        def find(stretches, k_pass, o):
            for j, (first, count) in enumerate(stretches):
                if first <= k_pass < first + count:
                    return j, (1 if first == 0 else 0) + 2 * (k_pass - first) + o

        acc = [acc_pool.tile([ITEMS, 2 * E], F32, name="acc%d" % p) for p in range(HOPS)]

        def load_scales(j, operands=(0, 1)):
            first, count = SCALE_STRETCHES[j]
            group = slice(first, first + count)
            view = w_planes[j][:, (1 if first == 0 else 0) :, :].rearrange("j (g o) n -> j g o n", o=2)
            for o in operands:
                for r in range(4):
                    nc.sync.dma_start(
                        out=view[r:P:32, :, o, :].bitcast(I32),
                        in_=dram_scales[o][group, r:16:4, :].bitcast(I32).rearrange("g q n -> q g n"),
                    )

        def load_words(j):
            first, count = WORD_STRETCHES[j]
            group = slice(first, first + count)
            view = w_words[j][:, (1 if first == 0 else 0) :, :].rearrange("j (g o) b -> j g o b", o=2)
            for o in range(2):
                nc.sync.dma_start(
                    out=view[:, :, o, :].bitcast(I32),
                    in_=dram_words[o][group].bitcast(I32).rearrange("g j b -> j g b"),
                )

        raw = {}

        def load_x(r):
            if r >= ROUNDS:
                return
            n = ROUND_PASSES[r]
            lo = ROUND_START[r] * K_PASS
            raw[r] = raw_pool.tile([P, HOPS, n * K_PASS], BF16, name="raw")
            nc.sync.dma_start(out=raw[r][:], in_=x[:, :, lo : lo + n * K_PASS])

        grouped = {}

        def turn(r):
            n = ROUND_PASSES[r]
            grouped[r] = grouped_pool.tile([P, HOPS, n, ITEMS, PACK], BF16, name="x_grouped", align_bytes=64)
            to = grouped[r][:].bitcast(F32)
            words = raw[r][:].bitcast(F32)
            for p in range(HOPS):
                turned = turn_pool.tile([P, n, 2, ITEMS], F32, name="turned")
                for g in range(n):
                    for u in range(2):
                        source = words[:, p, g * WORDS_PASS + u : (g + 1) * WORDS_PASS : 2]
                        nc.tensor.transpose(turned[:, g, u, :], source, identity[:])
                nc.scalar.copy(out=to[:, p], in_=turned[:].rearrange("j g u n -> j g n u"))

        codes = {}

        def quantise(flat, r, o, lo, hi):
            c, s = codes[r, o]
            nc.vector.quantize_mx(
                out=c[:, lo:hi].bitcast(FP8X4), scales=s[:, lo:hi], in_=flat[:, PACK * lo : PACK * hi]
            )

        def prepare(r):
            n = ROUND_PASSES[r]
            hop = n * ITEMS
            pair = pair_pool.tile([P, HOPS * hop * PACK], BF16, name="pair", align_bytes=64)
            for o in range(2):
                c = code_pool.tile([P, HOPS * hop], U32, name="codes%d" % o, align_bytes=64)
                s = code_pool.tile([P, HOPS * hop], U8, name="planes%d" % o, align_bytes=64)
                codes[r, o] = (c, s)
            own = grouped[r][:].rearrange("j p g n t -> j (p g n t)")
            w = hop * PACK
            quantise(own, r, 0, 0, 2 * hop)
            nc.vector.tensor_tensor(
                out=pair[:, 0 : 2 * w], in0=own[:, 0 : 2 * w], in1=own[:, w : 3 * w], op=ADD
            )
            nc.vector.tensor_tensor(
                out=pair[:, 2 * w :], in0=own[:, 2 * w :], in1=own[:, 0:w], op=ADD
            )
            quantise(own, r, 0, 2 * hop, 3 * hop)
            quantise(pair[:], r, 1, 0, 2 * hop)
            quantise(pair[:], r, 1, 2 * hop, 3 * hop)

        def multiply(r, o):
            n = ROUND_PASSES[r]
            c, s = codes[r, o]
            for slot in range(HOPS):
                p = slot if o == 0 else (slot + 2) % HOPS
                for g in range(n):
                    k_pass = ROUND_START[r] + g
                    lo = (slot * n + g) * ITEMS
                    own = slice(lo, lo + ITEMS)
                    jw, w = find(WORD_STRETCHES, k_pass, o)
                    jp, q = find(SCALE_STRETCHES, k_pass, o)
                    if k_pass == 0 and o == 0:
                        nc.tensor.matmul_mx(
                            out=acc[p][:],
                            lhsT=c[:, own].bitcast(FP8X4),
                            lhsT_scale=s[:, own],
                            rhs=w_words[0][:, 0:2, :].rearrange("j s b -> j (s b)").bitcast(FP4X4),
                            rhs_scale=w_planes[0][:, 0:2, :].rearrange("j s n -> j (s n)"),
                            start=True,
                            stop=False,
                        )
                        continue
                    for lo_n in range(0, E, N_MOVING):
                        at = lo_n + (E if o == 0 else 0)
                        nc.tensor.matmul_mx(
                            out=acc[p][:, at : at + N_MOVING],
                            lhsT=c[:, own].bitcast(FP8X4),
                            lhsT_scale=s[:, own],
                            rhs=w_words[jw][:, w, 2 * lo_n : 2 * (lo_n + N_MOVING)].bitcast(FP4X4),
                            rhs_scale=w_planes[jp][:, q, lo_n : lo_n + N_MOVING],
                            start=False,
                            stop=(k_pass == PASSES - 1 and o == 1 and lo_n + N_MOVING == E),
                        )

        load_x(0)
        load_x(1)
        load_x(2)
        load_x(3)
        load_words(0)
        load_scales(0)
        load_x(4)
        load_words(1)
        load_x(5)
        load_words(2)
        load_scales(1, (0,))
        load_x(6)
        load_scales(1, (1,))
        load_x(7)
        load_words(3)
        for step in range(ROUNDS + 2):
            if step < ROUNDS:
                turn(step)
            load_x(step + X_BUFS)
            if step % 2 == 0 and 4 <= step // 2 + 3 < len(WORD_STRETCHES):
                load_words(step // 2 + 3)
            if 0 <= step - 1 < ROUNDS:
                prepare(step - 1)
            for r in (0, 1) if step == 3 else (step - 2,) if step > 3 else ():
                multiply(r, 0)
                multiply(r, 1)

        out_rows = keep.tile([ITEMS, HOPS, E], F32, name="out_rows")
        for p in (2, 0, 1):
            own = end_pool.tile([ITEMS, E], F32, name="own")
            nc.scalar.copy(out=own[:], in_=acc[p][:, E : 2 * E])
            nc.vector.scalar_tensor_tensor(
                out=out_rows[:, p, :], in0=acc[p][:, 0:E], scalar=0.5, in1=own[:], op0=MULT, op1=ADD
            )
            nc.sync.dma_start(out=out[:, p, :], in_=out_rows[:, p, :])
